import numpy as np
import ml_dtypes

BF16 = ml_dtypes.bfloat16


def bf(x):
    return np.asarray(x, np.float32).astype(BF16)


def f32(x):
    return np.asarray(x, np.float32)


def f64(x):
    return np.asarray(x).astype(np.float64)


def striped(idx):
    return np.tile(idx.reshape(-1, 16).T, (8, 1))


D, S, N, NH, HD, KD, M = 128, 512, 256, 4, 64, 256, 512
EPS = 1e-5


def setup_inputs():
    return {
        "table": bf(np.random.standard_normal((D, S))),
        "w": bf(np.random.standard_normal((D, M)) / np.sqrt(D)),
        "b": f32(0.1 * np.random.standard_normal((M, 1))),
        "ln_w": f32(1.0 + 0.1 * np.random.standard_normal((HD, 1))),
        "ln_b": f32(0.1 * np.random.standard_normal((HD, 1))),
        "offs": striped(np.random.permutation(S)[:N]),
    }


def reference(table, w, b, ln_w, ln_b, offs):
    idx = offs[:16].T.reshape(-1)
    u = f64(w).T @ f64(table)[:, idx] + f64(b)
    k = u[:KD].reshape(NH, HD, N)
    mu = k.mean(axis=1, keepdims=True)
    var = np.square(k - mu).mean(axis=1, keepdims=True)
    kn = (k - mu) / np.sqrt(var + EPS) * f64(ln_w)[None] + f64(ln_b)[None]
    return np.concatenate([kn.reshape(KD, N), u[KD:]], axis=0)

@@ -1,0 +1,91 @@
+import concourse.mybir as mybir
+
+F32 = mybir.dt.float32
+BF16 = mybir.dt.bfloat16
+U16 = mybir.dt.uint16
+FUNC = mybir.ActivationFunctionType
+ALU = mybir.AluOpType
+
+P = 128
+S = 512
+N = 256
+M = 512
+HD = 64
+EPS = 1e-5
+BLOCKS = M // P
+KEY_BLOCKS = 2
+
+FLOPS = 2 * P * M * N
+BYTES = 2 * P * N + 2 * P * M + 4 * M + 2 * 4 * HD + 2 * P * (N // 16) + 4 * M * N
+
+
+def tile_persimmonattention_kernel(tc, table, w, b, ln_w, ln_b, offs, out):
+    nc = tc.nc
+    with (
+        tc.tile_pool(name="held", bufs=1) as held,
+        tc.psum_pool(name="psum", bufs=1) as psum,
+    ):
+        offsets = held.tile([P, N // 16], U16, name="offsets")
+        nc.sync.dma_start(offsets[:], offs)
+        table_sb = held.tile([P, S], BF16, name="table_sb")
+        nc.sync.dma_start(table_sb[:], table)
+        w_sb = held.tile([P, M], BF16, name="w_sb")
+        nc.scalar.dma_start(w_sb[:], w)
+
+        bias = held.tile([P, BLOCKS], F32, name="bias")
+        with nc.allow_non_contiguous_dma(reason="512 bias values, one to a partition and block"):
+            nc.scalar.dma_start(bias[:], b.rearrange("(c p) o -> p (c o)", p=P))
+        gain = held.tile([P, 1], F32, name="gain")
+        shift = held.tile([P, 1], F32, name="shift")
+        for h in range(P // HD):
+            nc.sync.dma_start(gain[h * HD : (h + 1) * HD, :], ln_w)
+            nc.sync.dma_start(shift[h * HD : (h + 1) * HD, :], ln_b)
+        eps = held.tile([P, 1], F32, name="eps")
+        nc.vector.memset(eps[:], EPS)
+
+        head_mean = held.tile([P, P], BF16, name="head_mean")
+        nc.gpsimd.memset(head_mean[:], 0.0)
+        for h in range(P // HD):
+            nc.gpsimd.memset(head_mean[h * HD : (h + 1) * HD, h * HD : (h + 1) * HD], 1.0 / HD)
+
+        for c in range(BLOCKS):
+            rows = out[c * P : (c + 1) * P, :]
+            bias_c = bias[:, c : c + 1]
+
+            u_ps = psum.tile([P, N], F32, name=f"u_ps{c}")
+            nc.tensor.matmul(
+                u_ps[:],
+                w_sb[:, c * P : (c + 1) * P],
+                table_sb[:].indirect(offsets[:]),
+                start=True,
+                stop=True,
+            )
+            u = held.tile([P, N], F32, name=f"u{c}")
+            nc.vector.tensor_scalar_add(u[:], u_ps[:], bias_c)
+            if c >= KEY_BLOCKS:
+                nc.sync.dma_start(rows, u[:])
+                continue
+
+            u_bf = held.tile([P, N], BF16, name=f"u_bf{c}")
+            nc.scalar.activation(u_bf[:], u_ps[:], FUNC.Identity, bias=bias_c)
+            mu_ps = psum.tile([P, N], F32, name=f"mu_ps{c}")
+            nc.tensor.matmul(mu_ps[:], head_mean[:], u_bf[:], start=True, stop=True)
+            centred = held.tile([P, N], F32, name=f"centred{c}")
+            nc.vector.tensor_sub(centred[:], u[:], mu_ps[:])
+
+            squares = held.tile([P, N], BF16, name=f"squares{c}")
+            nc.scalar.activation(squares[:], centred[:], FUNC.Square)
+            var_ps = psum.tile([P, N], F32, name=f"var_ps{c}")
+            nc.tensor.matmul(var_ps[:], head_mean[:], squares[:], start=True, stop=True)
+
+            std = held.tile([P, N], F32, name=f"std{c}")
+            nc.scalar.activation(std[:], var_ps[:], FUNC.Sqrt, bias=eps[:, 0:1])
+            rstd = held.tile([P, N], F32, name=f"rstd{c}")
+            nc.vector.reciprocal(rstd[:], std[:])
+            normed = held.tile([P, N], F32, name=f"normed{c}")
+            nc.vector.tensor_mul(normed[:], centred[:], rstd[:])
+            key = held.tile([P, N], F32, name=f"key{c}")
+            nc.vector.tensor_scalar(
+                key[:], normed[:], gain[:, 0:1], shift[:, 0:1], op0=ALU.mult, op1=ALU.add
+            )
+            nc.sync.dma_start(rows, key[:])

@@ -5,15 +5,17 @@ BF16 = mybir.dt.bfloat16
 U16 = mybir.dt.uint16
 FUNC = mybir.ActivationFunctionType
 ALU = mybir.AluOpType
+AXIS = mybir.AxisListType
 
 P = 128
 S = 512
 N = 256
 M = 512
+KD = 256
 HD = 64
 EPS = 1e-5
-BLOCKS = M // P
-KEY_BLOCKS = 2
+KEY_BLOCKS = KD // P
+VALUE_BLOCKS = (M - KD) // P
 
 FLOPS = 2 * P * M * N
 BYTES = 2 * P * N + 2 * P * M + 4 * M + 2 * 4 * HD + 2 * P * (N // 16) + 4 * M * N
@@ -25,67 +27,121 @@ def tile_persimmonattention_kernel(tc, table, w, b, ln_w, ln_b, offs, out):
         tc.tile_pool(name="held", bufs=1) as held,
         tc.psum_pool(name="psum", bufs=1) as psum,
     ):
-        offsets = held.tile([P, N // 16], U16, name="offsets")
-        nc.sync.dma_start(offsets[:], offs)
+        w_keys = held.tile([P, KD], BF16, name="w_keys")
+        nc.scalar.dma_start(w_keys[:], w[:, 0:KD])
         table_sb = held.tile([P, S], BF16, name="table_sb")
         nc.sync.dma_start(table_sb[:], table)
-        w_sb = held.tile([P, M], BF16, name="w_sb")
-        nc.scalar.dma_start(w_sb[:], w)
+        w_values = held.tile([P, M - KD], BF16, name="w_values")
+        nc.scalar.dma_start(w_values[:], w[:, KD:M])
+        offsets = held.tile([P, N // 16], U16, name="offsets")
+        nc.sync.dma_start(offsets[:], offs)
 
-        bias = held.tile([P, BLOCKS], F32, name="bias")
+        bias = held.tile([P, M // P], F32, name="bias")
         with nc.allow_non_contiguous_dma(reason="512 bias values, one to a partition and block"):
-            nc.scalar.dma_start(bias[:], b.rearrange("(c p) o -> p (c o)", p=P))
+            nc.sync.dma_start(bias[:], b.rearrange("(c p) o -> p (c o)", p=P))
+        head_bias = held.tile([P, KEY_BLOCKS, HD], F32, name="head_bias")
+        b_by_head = b[0:KD, :].rearrange("(c g e) o -> g o c e", g=P // HD, e=HD)
+        for g in range(P // HD):
+            nc.sync.dma_start(
+                head_bias[g * HD : (g + 1) * HD, :, :],
+                b_by_head[g].to_broadcast([HD, KEY_BLOCKS, HD]),
+            )
         gain = held.tile([P, 1], F32, name="gain")
         shift = held.tile([P, 1], F32, name="shift")
-        for h in range(P // HD):
-            nc.sync.dma_start(gain[h * HD : (h + 1) * HD, :], ln_w)
-            nc.sync.dma_start(shift[h * HD : (h + 1) * HD, :], ln_b)
+        for g in range(P // HD):
+            nc.sync.dma_start(gain[g * HD : (g + 1) * HD, :], ln_w)
+            nc.sync.dma_start(shift[g * HD : (g + 1) * HD, :], ln_b)
+
         eps = held.tile([P, 1], F32, name="eps")
         nc.vector.memset(eps[:], EPS)
+        warm = held.tile([P, 1], F32, name="warm")
+        nc.scalar.activation(warm[:], eps[:], FUNC.Abs_reciprocal_sqrt)
 
         head_mean = held.tile([P, P], BF16, name="head_mean")
         nc.gpsimd.memset(head_mean[:], 0.0)
-        for h in range(P // HD):
-            nc.gpsimd.memset(head_mean[h * HD : (h + 1) * HD, h * HD : (h + 1) * HD], 1.0 / HD)
+        for g in range(P // HD):
+            nc.gpsimd.memset(head_mean[g * HD : (g + 1) * HD, g * HD : (g + 1) * HD], 1.0 / HD)
 
-        for c in range(BLOCKS):
-            rows = out[c * P : (c + 1) * P, :]
-            bias_c = bias[:, c : c + 1]
+        w_sum = held.tile([P, KD // HD], F32, name="w_sum")
+        nc.vector.tensor_reduce(
+            w_sum[:], w_keys[:].rearrange("p (h e) -> p h e", e=HD), axis=AXIS.X, op=ALU.add
+        )
+        neg_mean_w = held.tile([P, KD], BF16, name="neg_mean_w")
+        nc.vector.tensor_scalar_mul(
+            neg_mean_w[:].rearrange("p (h e) -> p h e", e=HD),
+            w_sum[:].unsqueeze(2).to_broadcast([P, KD // HD, HD]),
+            -1.0 / HD,
+        )
 
-            u_ps = psum.tile([P, N], F32, name=f"u_ps{c}")
+        bias_sum = held.tile([P, KEY_BLOCKS], F32, name="bias_sum")
+        nc.vector.tensor_reduce(bias_sum[:], head_bias[:], axis=AXIS.X, op=ALU.add)
+        centred_bias = held.tile([P, KEY_BLOCKS], F32, name="centred_bias")
+        nc.vector.scalar_tensor_tensor(
+            centred_bias[:], bias_sum[:], -1.0 / HD, bias[:, 0:KEY_BLOCKS], op0=ALU.mult, op1=ALU.add
+        )
+
+        for c in range(VALUE_BLOCKS):
+            value_ps = psum.tile([P, N], F32, name=f"value_ps{c}")
             nc.tensor.matmul(
-                u_ps[:],
-                w_sb[:, c * P : (c + 1) * P],
+                value_ps[:],
+                w_values[:, c * P : (c + 1) * P],
                 table_sb[:].indirect(offsets[:]),
                 start=True,
                 stop=True,
             )
-            u = held.tile([P, N], F32, name=f"u{c}")
-            nc.vector.tensor_scalar_add(u[:], u_ps[:], bias_c)
-            if c >= KEY_BLOCKS:
-                nc.sync.dma_start(rows, u[:])
-                continue
+            value = held.tile([P, N], F32, name=f"value{c}")
+            nc.vector.tensor_scalar_add(
+                value[:], value_ps[:], bias[:, KEY_BLOCKS + c : KEY_BLOCKS + c + 1]
+            )
+            nc.sync.dma_start(out[KD + c * P : KD + (c + 1) * P, :], value[:])
 
-            u_bf = held.tile([P, N], BF16, name=f"u_bf{c}")
-            nc.scalar.activation(u_bf[:], u_ps[:], FUNC.Identity, bias=bias_c)
-            mu_ps = psum.tile([P, N], F32, name=f"mu_ps{c}")
-            nc.tensor.matmul(mu_ps[:], head_mean[:], u_bf[:], start=True, stop=True)
-            centred = held.tile([P, N], F32, name=f"centred{c}")
-            nc.vector.tensor_sub(centred[:], u[:], mu_ps[:])
+        centred_ps = [psum.tile([P, N], F32, name=f"centred_ps{c}") for c in range(KEY_BLOCKS)]
+        for c in range(KEY_BLOCKS):
+            nc.tensor.matmul(
+                centred_ps[c][:],
+                w_keys[:, c * P : (c + 1) * P],
+                table_sb[:].indirect(offsets[:]),
+                start=True,
+                stop=False,
+            )
+        for c in range(KEY_BLOCKS):
+            nc.tensor.matmul(
+                centred_ps[c][:],
+                neg_mean_w[:, c * P : (c + 1) * P],
+                table_sb[:].indirect(offsets[:]),
+                start=False,
+                stop=True,
+            )
 
+        rstd = []
+        for c in range(KEY_BLOCKS):
             squares = held.tile([P, N], BF16, name=f"squares{c}")
-            nc.scalar.activation(squares[:], centred[:], FUNC.Square)
+            nc.scalar.activation(
+                squares[:], centred_ps[c][:], FUNC.Square, bias=centred_bias[:, c : c + 1]
+            )
             var_ps = psum.tile([P, N], F32, name=f"var_ps{c}")
             nc.tensor.matmul(var_ps[:], head_mean[:], squares[:], start=True, stop=True)
+            rstd_c = held.tile([P, N], F32, name=f"rstd{c}")
+            nc.scalar.activation(rstd_c[:], var_ps[:], FUNC.Abs_reciprocal_sqrt, bias=eps[:, 0:1])
+            rstd.append(rstd_c)
 
-            std = held.tile([P, N], F32, name=f"std{c}")
-            nc.scalar.activation(std[:], var_ps[:], FUNC.Sqrt, bias=eps[:, 0:1])
-            rstd = held.tile([P, N], F32, name=f"rstd{c}")
-            nc.vector.reciprocal(rstd[:], std[:])
+        for c in range(KEY_BLOCKS):
             normed = held.tile([P, N], F32, name=f"normed{c}")
-            nc.vector.tensor_mul(normed[:], centred[:], rstd[:])
-            key = held.tile([P, N], F32, name=f"key{c}")
-            nc.vector.tensor_scalar(
-                key[:], normed[:], gain[:, 0:1], shift[:, 0:1], op0=ALU.mult, op1=ALU.add
+            nc.vector.scalar_tensor_tensor(
+                normed[:],
+                centred_ps[c][:],
+                centred_bias[:, c : c + 1],
+                rstd[c][:],
+                op0=ALU.add,
+                op1=ALU.mult,
             )
-            nc.sync.dma_start(rows, key[:])
+            key = held.tile([P, N], F32, name=f"key{c}")
+            if c < KEY_BLOCKS - 1:
+                nc.scalar.activation(
+                    key[:], normed[:], FUNC.Identity, bias=shift[:, 0:1], scale=gain[:, 0:1]
+                )
+            else:
+                nc.vector.tensor_scalar(
+                    key[:], normed[:], gain[:, 0:1], shift[:, 0:1], op0=ALU.mult, op1=ALU.add
+                )
+            nc.sync.dma_start(out[c * P : (c + 1) * P, :], key[:])

@@ -62,6 +62,12 @@ def tile_persimmonattention_kernel(tc, table, w, b, ln_w, ln_b, offs, out):
         for g in range(P // HD):
             nc.gpsimd.memset(head_mean[g * HD : (g + 1) * HD, g * HD : (g + 1) * HD], 1.0 / HD)
 
+        spin = held.tile([P, S], BF16, name="spin")
+        nc.vector.memset(spin[:], 0.0)
+        spin_ps = psum.tile([P, S], F32, name="spin_ps")
+        for i in range(4):
+            nc.tensor.matmul(spin_ps[:], spin[:, 0:P], spin[:], start=True, stop=True)
+
         w_sum = held.tile([P, KD // HD], F32, name="w_sum")
         nc.vector.tensor_reduce(
             w_sum[:], w_keys[:].rearrange("p (h e) -> p h e", e=HD), axis=AXIS.X, op=ALU.add

@@ -86,21 +86,6 @@ def tile_persimmonattention_kernel(tc, table, w, b, ln_w, ln_b, offs, out):
             centred_bias[:], bias_sum[:], -1.0 / HD, bias[:, 0:KEY_BLOCKS], op0=ALU.mult, op1=ALU.add
         )
 
-        for c in range(VALUE_BLOCKS):
-            value_ps = psum.tile([P, N], F32, name=f"value_ps{c}")
-            nc.tensor.matmul(
-                value_ps[:],
-                w_values[:, c * P : (c + 1) * P],
-                table_sb[:].indirect(offsets[:]),
-                start=True,
-                stop=True,
-            )
-            value = held.tile([P, N], F32, name=f"value{c}")
-            nc.vector.tensor_scalar_add(
-                value[:], value_ps[:], bias[:, KEY_BLOCKS + c : KEY_BLOCKS + c + 1]
-            )
-            nc.sync.dma_start(out[KD + c * P : KD + (c + 1) * P, :], value[:])
-
         centred_ps = [psum.tile([P, N], F32, name=f"centred_ps{c}") for c in range(KEY_BLOCKS)]
         for c in range(KEY_BLOCKS):
             nc.tensor.matmul(
@@ -118,6 +103,21 @@ def tile_persimmonattention_kernel(tc, table, w, b, ln_w, ln_b, offs, out):
                 start=False,
                 stop=True,
             )
+
+        for c in range(VALUE_BLOCKS):
+            value_ps = psum.tile([P, N], F32, name=f"value_ps{c}")
+            nc.tensor.matmul(
+                value_ps[:],
+                w_values[:, c * P : (c + 1) * P],
+                table_sb[:].indirect(offsets[:]),
+                start=True,
+                stop=True,
+            )
+            value = held.tile([P, N], F32, name=f"value{c}")
+            nc.vector.tensor_scalar_add(
+                value[:], value_ps[:], bias[:, KEY_BLOCKS + c : KEY_BLOCKS + c + 1]
+            )
+            nc.sync.dma_start(out[KD + c * P : KD + (c + 1) * P, :], value[:])
 
         rstd = []
         for c in range(KEY_BLOCKS):

@@ -28,17 +28,17 @@ def tile_persimmonattention_kernel(tc, table, w, b, ln_w, ln_b, offs, out):
         tc.psum_pool(name="psum", bufs=1) as psum,
     ):
         w_keys = held.tile([P, KD], BF16, name="w_keys")
-        nc.scalar.dma_start(w_keys[:], w[:, 0:KD])
+        nc.sync.dma_start(w_keys[:], w[:, 0:KD])
         table_sb = held.tile([P, S], BF16, name="table_sb")
         nc.sync.dma_start(table_sb[:], table)
-        w_values = held.tile([P, M - KD], BF16, name="w_values")
-        nc.scalar.dma_start(w_values[:], w[:, KD:M])
         offsets = held.tile([P, N // 16], U16, name="offsets")
         nc.sync.dma_start(offsets[:], offs)
+        w_values = held.tile([P, M - KD], BF16, name="w_values")
+        nc.scalar.dma_start(w_values[:], w[:, KD:M])
 
-        bias = held.tile([P, M // P], F32, name="bias")
-        with nc.allow_non_contiguous_dma(reason="512 bias values, one to a partition and block"):
-            nc.sync.dma_start(bias[:], b.rearrange("(c p) o -> p (c o)", p=P))
+        key_bias = held.tile([P, KEY_BLOCKS], F32, name="key_bias")
+        with nc.allow_non_contiguous_dma(reason="256 bias values, one to a partition and block"):
+            nc.sync.dma_start(key_bias[:], b[0:KD, :].rearrange("(c p) o -> p (c o)", p=P))
         head_bias = held.tile([P, KEY_BLOCKS, HD], F32, name="head_bias")
         b_by_head = b[0:KD, :].rearrange("(c g e) o -> g o c e", g=P // HD, e=HD)
         for g in range(P // HD):
@@ -46,6 +46,9 @@ def tile_persimmonattention_kernel(tc, table, w, b, ln_w, ln_b, offs, out):
                 head_bias[g * HD : (g + 1) * HD, :, :],
                 b_by_head[g].to_broadcast([HD, KEY_BLOCKS, HD]),
             )
+        value_bias = held.tile([P, VALUE_BLOCKS], F32, name="value_bias")
+        with nc.allow_non_contiguous_dma(reason="256 bias values, one to a partition and block"):
+            nc.sync.dma_start(value_bias[:], b[KD:M, :].rearrange("(c p) o -> p (c o)", p=P))
         gain = held.tile([P, 1], F32, name="gain")
         shift = held.tile([P, 1], F32, name="shift")
         for g in range(P // HD):
@@ -83,7 +86,7 @@ def tile_persimmonattention_kernel(tc, table, w, b, ln_w, ln_b, offs, out):
         nc.vector.tensor_reduce(bias_sum[:], head_bias[:], axis=AXIS.X, op=ALU.add)
         centred_bias = held.tile([P, KEY_BLOCKS], F32, name="centred_bias")
         nc.vector.scalar_tensor_tensor(
-            centred_bias[:], bias_sum[:], -1.0 / HD, bias[:, 0:KEY_BLOCKS], op0=ALU.mult, op1=ALU.add
+            centred_bias[:], bias_sum[:], -1.0 / HD, key_bias[:], op0=ALU.mult, op1=ALU.add
         )
 
         centred_ps = [psum.tile([P, N], F32, name=f"centred_ps{c}") for c in range(KEY_BLOCKS)]
@@ -115,7 +118,7 @@ def tile_persimmonattention_kernel(tc, table, w, b, ln_w, ln_b, offs, out):
             )
             value = held.tile([P, N], F32, name=f"value{c}")
             nc.vector.tensor_scalar_add(
-                value[:], value_ps[:], bias[:, KEY_BLOCKS + c : KEY_BLOCKS + c + 1]
+                value[:], value_ps[:], value_bias[:, c : c + 1]
             )
             nc.sync.dma_start(out[KD + c * P : KD + (c + 1) * P, :], value[:])
 

@@ -28,13 +28,13 @@ def tile_persimmonattention_kernel(tc, table, w, b, ln_w, ln_b, offs, out):
         tc.psum_pool(name="psum", bufs=1) as psum,
     ):
         w_keys = held.tile([P, KD], BF16, name="w_keys")
-        nc.sync.dma_start(w_keys[:], w[:, 0:KD])
+        nc.scalar.dma_start(w_keys[:], w[:, 0:KD])
         table_sb = held.tile([P, S], BF16, name="table_sb")
         nc.sync.dma_start(table_sb[:], table)
-        offsets = held.tile([P, N // 16], U16, name="offsets")
-        nc.sync.dma_start(offsets[:], offs)
         w_values = held.tile([P, M - KD], BF16, name="w_values")
         nc.scalar.dma_start(w_values[:], w[:, KD:M])
+        offsets = held.tile([P, N // 16], U16, name="offsets")
+        nc.sync.dma_start(offsets[:], offs)
 
         key_bias = held.tile([P, KEY_BLOCKS], F32, name="key_bias")
         with nc.allow_non_contiguous_dma(reason="256 bias values, one to a partition and block"):

@@ -65,12 +65,6 @@ def tile_persimmonattention_kernel(tc, table, w, b, ln_w, ln_b, offs, out):
         for g in range(P // HD):
             nc.gpsimd.memset(head_mean[g * HD : (g + 1) * HD, g * HD : (g + 1) * HD], 1.0 / HD)
 
-        spin = held.tile([P, S], BF16, name="spin")
-        nc.vector.memset(spin[:], 0.0)
-        spin_ps = psum.tile([P, S], F32, name="spin_ps")
-        for i in range(4):
-            nc.tensor.matmul(spin_ps[:], spin[:, 0:P], spin[:], start=True, stop=True)
-
         w_sum = held.tile([P, KD // HD], F32, name="w_sum")
         nc.vector.tensor_reduce(
             w_sum[:], w_keys[:].rearrange("p (h e) -> p h e", e=HD), axis=AXIS.X, op=ALU.add

@@ -76,12 +76,18 @@ def tile_persimmonattention_kernel(tc, table, w, b, ln_w, ln_b, offs, out):
             -1.0 / HD,
         )
 
-        bias_sum = held.tile([P, KEY_BLOCKS], F32, name="bias_sum")
-        nc.vector.tensor_reduce(bias_sum[:], head_bias[:], axis=AXIS.X, op=ALU.add)
         centred_bias = held.tile([P, KEY_BLOCKS], F32, name="centred_bias")
-        nc.vector.scalar_tensor_tensor(
-            centred_bias[:], bias_sum[:], -1.0 / HD, key_bias[:], op0=ALU.mult, op1=ALU.add
-        )
+        for c in range(KEY_BLOCKS):
+            products = held.tile([P, HD], F32, name=f"products{c}")
+            nc.vector.tensor_scalar(
+                products[:],
+                head_bias[:, c, :],
+                -1.0 / HD,
+                key_bias[:, c : c + 1],
+                op0=ALU.mult,
+                op1=ALU.add,
+                accum_out=centred_bias[:, c : c + 1],
+            )
 
         centred_ps = [psum.tile([P, N], F32, name=f"centred_ps{c}") for c in range(KEY_BLOCKS)]
         for c in range(KEY_BLOCKS):

@@ -16,6 +16,7 @@ HD = 64
 EPS = 1e-5
 KEY_BLOCKS = KD // P
 VALUE_BLOCKS = (M - KD) // P
+PIECE = 128
 
 FLOPS = 2 * P * M * N
 BYTES = 2 * P * N + 2 * P * M + 4 * M + 2 * 4 * HD + 2 * P * (N // 16) + 4 * M * N
@@ -122,35 +123,38 @@ def tile_persimmonattention_kernel(tc, table, w, b, ln_w, ln_b, offs, out):
             )
             nc.sync.dma_start(out[KD + c * P : KD + (c + 1) * P, :], value[:])
 
-        rstd = []
-        for c in range(KEY_BLOCKS):
-            squares = held.tile([P, N], BF16, name=f"squares{c}")
-            nc.scalar.activation(
-                squares[:], centred_ps[c][:], FUNC.Square, bias=centred_bias[:, c : c + 1]
-            )
-            var_ps = psum.tile([P, N], F32, name=f"var_ps{c}")
-            nc.tensor.matmul(var_ps[:], head_mean[:], squares[:], start=True, stop=True)
-            rstd_c = held.tile([P, N], F32, name=f"rstd{c}")
-            nc.scalar.activation(rstd_c[:], var_ps[:], FUNC.Abs_reciprocal_sqrt, bias=eps[:, 0:1])
-            rstd.append(rstd_c)
+        pieces = [(c, slice(j, j + PIECE)) for c in range(KEY_BLOCKS) for j in range(0, N, PIECE)]
 
-        for c in range(KEY_BLOCKS):
-            normed = held.tile([P, N], F32, name=f"normed{c}")
+        rstd = []
+        for i, (c, cols) in enumerate(pieces):
+            squares = held.tile([P, PIECE], BF16, name=f"squares{i}")
+            nc.scalar.activation(
+                squares[:], centred_ps[c][:, cols], FUNC.Square, bias=centred_bias[:, c : c + 1]
+            )
+            var_ps = psum.tile([P, PIECE], F32, name=f"var_ps{i}")
+            nc.tensor.matmul(var_ps[:], head_mean[:], squares[:], start=True, stop=True)
+            rstd_i = held.tile([P, PIECE], F32, name=f"rstd{i}")
+            nc.scalar.activation(rstd_i[:], var_ps[:], FUNC.Abs_reciprocal_sqrt, bias=eps[:, 0:1])
+            rstd.append(rstd_i)
+
+        key = [held.tile([P, N], F32, name=f"key{c}") for c in range(KEY_BLOCKS)]
+        for i, (c, cols) in enumerate(pieces):
+            normed = held.tile([P, PIECE], F32, name=f"normed{i}")
             nc.vector.scalar_tensor_tensor(
                 normed[:],
-                centred_ps[c][:],
+                centred_ps[c][:, cols],
                 centred_bias[:, c : c + 1],
-                rstd[c][:],
+                rstd[i][:],
                 op0=ALU.add,
                 op1=ALU.mult,
             )
-            key = held.tile([P, N], F32, name=f"key{c}")
             if c < KEY_BLOCKS - 1:
                 nc.scalar.activation(
-                    key[:], normed[:], FUNC.Identity, bias=shift[:, 0:1], scale=gain[:, 0:1]
+                    key[c][:, cols], normed[:], FUNC.Identity, bias=shift[:, 0:1], scale=gain[:, 0:1]
                 )
             else:
                 nc.vector.tensor_scalar(
-                    key[:], normed[:], gain[:, 0:1], shift[:, 0:1], op0=ALU.mult, op1=ALU.add
+                    key[c][:, cols], normed[:], gain[:, 0:1], shift[:, 0:1], op0=ALU.mult, op1=ALU.add
                 )
-            nc.sync.dma_start(out[c * P : (c + 1) * P, :], key[:])
+        for c in range(KEY_BLOCKS):
+            nc.sync.dma_start(out[c * P : (c + 1) * P, :], key[c][:])

@@ -66,15 +66,17 @@ def tile_persimmonattention_kernel(tc, table, w, b, ln_w, ln_b, offs, out):
         for g in range(P // HD):
             nc.gpsimd.memset(head_mean[g * HD : (g + 1) * HD, g * HD : (g + 1) * HD], 1.0 / HD)
 
+        w_by_head = w_keys[:].rearrange("p (h e) -> p h e", e=HD)
         w_sum = held.tile([P, KD // HD], F32, name="w_sum")
-        nc.vector.tensor_reduce(
-            w_sum[:], w_keys[:].rearrange("p (h e) -> p h e", e=HD), axis=AXIS.X, op=ALU.add
-        )
-        neg_mean_w = held.tile([P, KD], BF16, name="neg_mean_w")
-        nc.vector.tensor_scalar_mul(
-            neg_mean_w[:].rearrange("p (h e) -> p h e", e=HD),
+        nc.vector.tensor_reduce(w_sum[:], w_by_head, axis=AXIS.X, op=ALU.add)
+        centred_w = held.tile([P, KD], BF16, name="centred_w")
+        nc.vector.scalar_tensor_tensor(
+            centred_w[:].rearrange("p (h e) -> p h e", e=HD),
             w_sum[:].unsqueeze(2).to_broadcast([P, KD // HD, HD]),
             -1.0 / HD,
+            w_by_head,
+            op0=ALU.mult,
+            op1=ALU.add,
         )
 
         centred_bias = held.tile([P, KEY_BLOCKS], F32, name="centred_bias")
@@ -90,37 +92,29 @@ def tile_persimmonattention_kernel(tc, table, w, b, ln_w, ln_b, offs, out):
                 accum_out=centred_bias[:, c : c + 1],
             )
 
-        centred_ps = [psum.tile([P, N], F32, name=f"centred_ps{c}") for c in range(KEY_BLOCKS)]
-        for c in range(KEY_BLOCKS):
-            nc.tensor.matmul(
-                centred_ps[c][:],
-                w_keys[:, c * P : (c + 1) * P],
-                table_sb[:].indirect(offsets[:]),
-                start=True,
-                stop=False,
-            )
-        for c in range(KEY_BLOCKS):
-            nc.tensor.matmul(
-                centred_ps[c][:],
-                neg_mean_w[:, c * P : (c + 1) * P],
-                table_sb[:].indirect(offsets[:]),
-                start=False,
-                stop=True,
-            )
-
+        value_ps = [psum.tile([P, N], F32, name=f"value_ps{c}") for c in range(VALUE_BLOCKS)]
         for c in range(VALUE_BLOCKS):
-            value_ps = psum.tile([P, N], F32, name=f"value_ps{c}")
             nc.tensor.matmul(
-                value_ps[:],
+                value_ps[c][:],
                 w_values[:, c * P : (c + 1) * P],
                 table_sb[:].indirect(offsets[:]),
                 start=True,
                 stop=True,
             )
-            value = held.tile([P, N], F32, name=f"value{c}")
-            nc.vector.tensor_scalar_add(
-                value[:], value_ps[:], value_bias[:, c : c + 1]
+
+        centred_ps = [psum.tile([P, N], F32, name=f"centred_ps{c}") for c in range(KEY_BLOCKS)]
+        for c in range(KEY_BLOCKS):
+            nc.tensor.matmul(
+                centred_ps[c][:],
+                centred_w[:, c * P : (c + 1) * P],
+                table_sb[:].indirect(offsets[:]),
+                start=True,
+                stop=True,
             )
+
+        for c in range(VALUE_BLOCKS):
+            value = held.tile([P, N], F32, name=f"value{c}")
+            nc.vector.tensor_scalar_add(value[:], value_ps[c][:], value_bias[:, c : c + 1])
             nc.sync.dma_start(out[KD + c * P : KD + (c + 1) * P, :], value[:])
 
         pieces = [(c, slice(j, j + PIECE)) for c in range(KEY_BLOCKS) for j in range(0, N, PIECE)]

import concourse.mybir as mybir

F32 = mybir.dt.float32
BF16 = mybir.dt.bfloat16
U16 = mybir.dt.uint16
FUNC = mybir.ActivationFunctionType
ALU = mybir.AluOpType
AXIS = mybir.AxisListType

P = 128
S = 512
N = 256
M = 512
KD = 256
HD = 64
EPS = 1e-5
KEY_BLOCKS = KD // P
VALUE_BLOCKS = (M - KD) // P
PIECE = 128

FLOPS = 2 * P * M * N
BYTES = 2 * P * N + 2 * P * M + 4 * M + 2 * 4 * HD + 2 * P * (N // 16) + 4 * M * N


def tile_persimmonattention_kernel(tc, table, w, b, ln_w, ln_b, offs, out):
    nc = tc.nc
    with (
        tc.tile_pool(name="held", bufs=1) as held,
        tc.psum_pool(name="psum", bufs=1) as psum,
    ):
        w_keys = held.tile([P, KD], BF16, name="w_keys")
        nc.scalar.dma_start(w_keys[:], w[:, 0:KD])
        table_sb = held.tile([P, S], BF16, name="table_sb")
        nc.sync.dma_start(table_sb[:], table)
        w_values = held.tile([P, M - KD], BF16, name="w_values")
        nc.scalar.dma_start(w_values[:], w[:, KD:M])
        offsets = held.tile([P, N // 16], U16, name="offsets")
        nc.sync.dma_start(offsets[:], offs)

        key_bias = held.tile([P, KEY_BLOCKS], F32, name="key_bias")
        with nc.allow_non_contiguous_dma(reason="256 bias values, one to a partition and block"):
            nc.sync.dma_start(key_bias[:], b[0:KD, :].rearrange("(c p) o -> p (c o)", p=P))
        head_bias = held.tile([P, KEY_BLOCKS, HD], F32, name="head_bias")
        b_by_head = b[0:KD, :].rearrange("(c g e) o -> g o c e", g=P // HD, e=HD)
        for g in range(P // HD):
            nc.sync.dma_start(
                head_bias[g * HD : (g + 1) * HD, :, :],
                b_by_head[g].to_broadcast([HD, KEY_BLOCKS, HD]),
            )
        value_bias = held.tile([P, VALUE_BLOCKS], F32, name="value_bias")
        with nc.allow_non_contiguous_dma(reason="256 bias values, one to a partition and block"):
            nc.sync.dma_start(value_bias[:], b[KD:M, :].rearrange("(c p) o -> p (c o)", p=P))
        gain = held.tile([P, 1], F32, name="gain")
        shift = held.tile([P, 1], F32, name="shift")
        for g in range(P // HD):
            nc.sync.dma_start(gain[g * HD : (g + 1) * HD, :], ln_w)
            nc.sync.dma_start(shift[g * HD : (g + 1) * HD, :], ln_b)

        eps = held.tile([P, 1], F32, name="eps")
        nc.vector.memset(eps[:], EPS)
        warm = held.tile([P, 1], F32, name="warm")
        nc.scalar.activation(warm[:], eps[:], FUNC.Abs_reciprocal_sqrt)

        head_mean = held.tile([P, P], BF16, name="head_mean")
        nc.gpsimd.memset(head_mean[:], 0.0)
        for g in range(P // HD):
            nc.gpsimd.memset(head_mean[g * HD : (g + 1) * HD, g * HD : (g + 1) * HD], 1.0 / HD)

        w_by_head = w_keys[:].rearrange("p (h e) -> p h e", e=HD)
        w_sum = held.tile([P, KD // HD], F32, name="w_sum")
        nc.vector.tensor_reduce(w_sum[:], w_by_head, axis=AXIS.X, op=ALU.add)
        centred_w = held.tile([P, KD], BF16, name="centred_w")
        nc.vector.scalar_tensor_tensor(
            centred_w[:].rearrange("p (h e) -> p h e", e=HD),
            w_sum[:].unsqueeze(2).to_broadcast([P, KD // HD, HD]),
            -1.0 / HD,
            w_by_head,
            op0=ALU.mult,
            op1=ALU.add,
        )

        centred_bias = held.tile([P, KEY_BLOCKS], F32, name="centred_bias")
        for c in range(KEY_BLOCKS):
            products = held.tile([P, HD], F32, name=f"products{c}")
            nc.vector.tensor_scalar(
                products[:],
                head_bias[:, c, :],
                -1.0 / HD,
                key_bias[:, c : c + 1],
                op0=ALU.mult,
                op1=ALU.add,
                accum_out=centred_bias[:, c : c + 1],
            )

        value_ps = [psum.tile([P, N], F32, name=f"value_ps{c}") for c in range(VALUE_BLOCKS)]
        for c in range(VALUE_BLOCKS):
            nc.tensor.matmul(
                value_ps[c][:],
                w_values[:, c * P : (c + 1) * P],
                table_sb[:].indirect(offsets[:]),
                start=True,
                stop=True,
            )

        centred_ps = [psum.tile([P, N], F32, name=f"centred_ps{c}") for c in range(KEY_BLOCKS)]
        for c in range(KEY_BLOCKS):
            nc.tensor.matmul(
                centred_ps[c][:],
                centred_w[:, c * P : (c + 1) * P],
                table_sb[:].indirect(offsets[:]),
                start=True,
                stop=True,
            )

        for c in range(VALUE_BLOCKS):
            value = held.tile([P, N], F32, name=f"value{c}")
            nc.vector.tensor_scalar_add(value[:], value_ps[c][:], value_bias[:, c : c + 1])
            nc.sync.dma_start(out[KD + c * P : KD + (c + 1) * P, :], value[:])

        pieces = [(c, slice(j, j + PIECE)) for c in range(KEY_BLOCKS) for j in range(0, N, PIECE)]

        rstd = []
        for i, (c, cols) in enumerate(pieces):
            squares = held.tile([P, PIECE], BF16, name=f"squares{i}")
            nc.scalar.activation(
                squares[:], centred_ps[c][:, cols], FUNC.Square, bias=centred_bias[:, c : c + 1]
            )
            var_ps = psum.tile([P, PIECE], F32, name=f"var_ps{i}")
            nc.tensor.matmul(var_ps[:], head_mean[:], squares[:], start=True, stop=True)
            rstd_i = held.tile([P, PIECE], F32, name=f"rstd{i}")
            nc.scalar.activation(rstd_i[:], var_ps[:], FUNC.Abs_reciprocal_sqrt, bias=eps[:, 0:1])
            rstd.append(rstd_i)

        key = [held.tile([P, N], F32, name=f"key{c}") for c in range(KEY_BLOCKS)]
        for i, (c, cols) in enumerate(pieces):
            normed = held.tile([P, PIECE], F32, name=f"normed{i}")
            nc.vector.scalar_tensor_tensor(
                normed[:],
                centred_ps[c][:, cols],
                centred_bias[:, c : c + 1],
                rstd[i][:],
                op0=ALU.add,
                op1=ALU.mult,
            )
            if c < KEY_BLOCKS - 1:
                nc.scalar.activation(
                    key[c][:, cols], normed[:], FUNC.Identity, bias=shift[:, 0:1], scale=gain[:, 0:1]
                )
            else:
                nc.vector.tensor_scalar(
                    key[c][:, cols], normed[:], gain[:, 0:1], shift[:, 0:1], op0=ALU.mult, op1=ALU.add
                )
        for c in range(KEY_BLOCKS):
            nc.sync.dma_start(out[c * P : (c + 1) * P, :], key[c][:])
